import numpy as np
import ml_dtypes


def mxq(x, axis, fmt="e4m3"):
    dtype, down = {"e4m3": (ml_dtypes.float8_e4m3fn, 7), "e5m2": (ml_dtypes.float8_e5m2, 14)}[fmt]
    v = np.moveaxis(np.asarray(x, np.float32).astype(ml_dtypes.bfloat16).astype(np.float64), axis, -1)
    blocks = v.reshape(v.shape[:-1] + (-1, 32))
    amax = np.abs(blocks).max(-1, keepdims=True)
    byte = np.maximum(np.where(amax > 0, np.frexp(amax)[1] - 1 + 127, 0) - down, 1)
    scale = np.exp2(byte - 127.0)
    codes = (blocks / scale).astype(np.float32).astype(dtype).astype(np.float64)
    return np.moveaxis((codes * scale).reshape(v.shape), -1, axis)


WIDE = False


def mx_kscale(k):
    if not WIDE:
        return np.ones(k)
    levels = np.array([10, -10, 5, -5, 0])
    a = np.random.permutation(np.resize(levels, k // 512 * 4)).reshape(k // 512, 4)
    idx = np.arange(k)
    return np.exp2(a[idx // 512, idx % 128 // 32])


BF16 = ml_dtypes.bfloat16


def bf(x):
    return np.asarray(x, np.float32).astype(BF16)


def f64(x):
    return np.asarray(x).astype(np.float64)


E2M1 = np.array([0.0, 0.5, 1.0, 1.5, 2.0, 3.0, 4.0, 6.0, -0.0, -0.5, -1.0, -1.5, -2.0, -3.0, -4.0, -6.0])


def pack_weight(w, fmt):
    k, n = w.shape
    w = f64(bf(w)).reshape(k // 32, 32, n)
    amax = np.abs(w).max(1)
    if fmt == "e4m3":
        byte = np.frexp(amax)[1] - 1 + 127 - 7
    else:
        mant, ex = np.frexp(amax / 6.0)
        byte = np.where(mant > 0.5, ex, ex - 1) + 127
    byte = np.clip(np.where(amax > 0, byte, 1), 1, 254)
    scaled = (w * np.exp2(127.0 - byte)[:, None, :]).reshape(k, n).astype(np.float32)
    by_word = np.ascontiguousarray(scaled.reshape(k // 512, 128, 4, n).transpose(0, 1, 3, 2))
    if fmt == "e4m3":
        words = by_word.astype(ml_dtypes.float8_e4m3fn).view(np.uint8)
    else:
        c = by_word.astype(ml_dtypes.float4_e2m1fn).view(np.uint8) & 0xF
        words = c[..., 0::2] | (c[..., 1::2] << 4)
    return np.ascontiguousarray(words), np.ascontiguousarray(byte.astype(np.uint8).reshape(k // 512, 16, n))


def unpack_weight(words, scales, fmt):
    g, p, n, _ = words.shape
    if fmt == "e4m3":
        vals = np.ascontiguousarray(words).view(ml_dtypes.float8_e4m3fn).astype(np.float64)
    else:
        nib = np.empty((g, p, n, 4), np.uint8)
        nib[..., 0::2] = words & 0xF
        nib[..., 1::2] = words >> 4
        vals = E2M1[nib]
    vals = vals * np.repeat(np.exp2(scales.astype(np.float64) - 127.0), 8, axis=1)[..., None]
    return vals.transpose(0, 1, 3, 2).reshape(g * 512, n)

def pack4(w):
    words, scales = pack_weight(w, "e2m1")
    return words.reshape(words.shape[0], 128, -1), scales


def unpack4(words, scales):
    return unpack_weight(words.reshape(words.shape[0], 128, -1, 2), scales, "e2m1")


B, S, D, H = 2, 512, 1024, 8
DH = D // H


def softmax(v, axis):
    e = np.exp(v - v.max(axis, keepdims=True))
    return e / e.sum(axis, keepdims=True)


def setup_inputs():
    t = mx_kscale(D)[:DH]
    q_soft = bf(softmax(np.random.standard_normal((B, H, S, DH)) * 1.5, -1))
    kv = bf(np.random.standard_normal((B, H, DH, DH)) * 6.0 * np.sqrt(S) / DH * t)
    w = np.random.standard_normal((D, H * DH)) * 2.0 / np.sqrt(D) / np.tile(t, H)
    words, scales = pack4(np.ascontiguousarray(w.T))
    return {"q_soft": q_soft,
            "kv": kv,
            "W_O_words": words,
            "W_O_scales": scales}


def reference(q_soft, kv, W_O_words, W_O_scales):
    bt = f64(q_soft) @ f64(kv)
    y = bt.reshape(B, S, H * DH)
    return mxq(y, 2, "e4m3") @ unpack4(W_O_words, W_O_scales)

@@ -1,0 +1,154 @@
+from contextlib import ExitStack
+
+import concourse.mybir as mybir
+from concourse.masks import make_identity
+
+BF16 = mybir.dt.bfloat16
+F32 = mybir.dt.float32
+I32 = mybir.dt.int32
+U8 = mybir.dt.uint8
+U32 = mybir.dt.uint32
+FP8X4 = mybir.dt.float8_e4m3fn_x4
+FP4X4 = mybir.dt.float4_e2m1fn_x4
+
+B, H, S, DH = 2, 8, 512, 128
+D = H * DH
+
+P = 128
+PACK = 4
+PASSES = D // (P * PACK)
+SQUARE = 32
+HEADS = B * H
+TILE_HEADS = 2
+ROW_TILES = HEADS // TILE_HEADS
+ROW_GROUPS = S // 8 // SQUARE
+N_TILE = 512
+N_TILES = D // N_TILE
+AHEAD = 2
+
+FLOPS = 2 * B * H * S * DH * DH + 2 * B * S * D * D
+
+
+def tile_mhla2_pb_kernel(tc, q_soft, kv, W_O_words, W_O_scales, out):
+    nc = tc.nc
+    q_rows = q_soft.rearrange("b h (a x) d -> a (b h) x d", x=PACK)
+    out_rows = out.rearrange("b r o -> (b r) o")
+
+    with ExitStack() as ctx:
+        keep = ctx.enter_context(tc.tile_pool(name="keep", bufs=1))
+        stage = ctx.enter_context(tc.tile_pool(name="stage", bufs=3))
+        results = ctx.enter_context(tc.tile_pool(name="results", bufs=4))
+        banks = ctx.enter_context(tc.psum_pool(name="banks", bufs=8))
+        ctx.enter_context(tc.manual_schedule())
+
+        q_sb = keep.tile([P, HEADS, PACK, DH], BF16)
+        for rt in range(ROW_TILES):
+            heads = slice(TILE_HEADS * rt, TILE_HEADS * (rt + 1))
+            nc.sync.dma_start(out=q_sb[:, heads], in_=q_rows[:, heads])
+        kv_sb = keep.tile([P, HEADS, DH], BF16)
+        for b in range(B):
+            nc.scalar.dma_start(out=kv_sb[:, H * b : H * (b + 1), :], in_=kv[b].rearrange("h d e -> d h e"))
+
+        w_words = keep.tile([P, PASSES, 2 * D], U8, align_bytes=64)
+        nc.sync.dma_start(out=w_words[:].bitcast(I32), in_=W_O_words.bitcast(I32).rearrange("g p n -> p g n"))
+        w_scales = keep.tile([P, PASSES, D], U8, align_bytes=64)
+        nc.vector.memset(w_scales[:].bitcast(I32), 0)
+        scale_rows = W_O_scales.bitcast(I32).rearrange("g q n -> q g n")
+        for quadrant in range(P // SQUARE):
+            nc.sync.dma_start(
+                out=w_scales[SQUARE * quadrant : SQUARE * quadrant + PACK].bitcast(I32),
+                in_=scale_rows[PACK * quadrant : PACK * (quadrant + 1)],
+            )
+
+        identity = keep.tile([P, P], BF16)
+        make_identity(nc, identity[:])
+        order = keep.tile([P, P], BF16)
+        nc.vector.tensor_copy(
+            out=order[:].rearrange("a (g j i) -> a g j i", g=PASSES, j=ROW_GROUPS),
+            in_=identity[:].rearrange("a (j i g) -> a g j i", g=PASSES, j=ROW_GROUPS),
+        )
+
+        kv_pairs = keep.tile([P, HEADS, DH], BF16)
+        y_codes = keep.tile([P, ROW_TILES, PASSES * P], U32, align_bytes=64)
+        y_scales = keep.tile([P, ROW_TILES, PASSES * P], U8, align_bytes=64)
+        q_t = {}
+        grouped = {}
+
+        def order_kv(b):
+            heads = slice(H * b, H * (b + 1))
+            nc.vector.tensor_copy(
+                out=kv_pairs[:, heads, :].bitcast(F32).rearrange("d h (u c) -> d h u c", u=2),
+                in_=kv_sb[:, heads, :].bitcast(F32).rearrange("d h (c u) -> d h u c", u=2),
+            )
+
+        def transpose_q(rt):
+            q_t_ps = banks.tile([P, TILE_HEADS, PASSES * ROW_GROUPS, PACK, SQUARE], BF16, tag="bank")
+            for h in range(TILE_HEADS):
+                for x in range(PACK):
+                    nc.tensor.transpose(
+                        out=q_t_ps[:, h, :, x, :],
+                        in_=q_sb[:, TILE_HEADS * rt + h, x, :],
+                        identity=order[:],
+                    )
+            q_t[rt] = stage.tile([P, TILE_HEADS, PASSES * ROW_GROUPS, P], BF16, name="q_t_sb")
+            nc.scalar.copy(
+                out=q_t[rt][:].rearrange("d h o m -> d (h o m)"),
+                in_=q_t_ps[:].rearrange("d h o x i -> d (h o x i)"),
+            )
+
+        def read_out(rt):
+            y_ps = banks.tile([P, PASSES, TILE_HEADS, ROW_GROUPS, DH], BF16, tag="bank")
+            for h in range(TILE_HEADS):
+                for g in range(PASSES):
+                    for j in range(ROW_GROUPS):
+                        nc.tensor.matmul(
+                            out=y_ps[:, g, h, j, :],
+                            lhsT=q_t[rt][:, h, ROW_GROUPS * g + j, :],
+                            rhs=kv_pairs[:, TILE_HEADS * rt + h, :],
+                            start=True,
+                            stop=True,
+                        )
+            turned = stage.tile([P, PASSES * P * 2], F32, align_bytes=64)
+            nc.vector.transpose(out=turned[:], in_=y_ps[:].rearrange("m g h j n -> m (g h j n)").bitcast(F32))
+            grouped[rt] = stage.tile([P, PASSES * P * PACK], BF16, name="grouped", align_bytes=64)
+            nc.vector.tensor_copy(
+                out=grouped[rt][:].bitcast(F32).rearrange("p (o i u) -> p o i u", i=SQUARE, u=2),
+                in_=turned[:].rearrange("p (o u i) -> p o i u", i=SQUARE, u=2),
+            )
+
+        def quantise(rt):
+            nc.vector.quantize_mx(
+                out=y_codes[:, rt, :].bitcast(FP8X4), scales=y_scales[:, rt, :], in_=grouped[rt][:]
+            )
+
+        def project(rt):
+            out_sb = results.tile([P, D], F32)
+            for n in range(N_TILES):
+                out_ps = banks.tile([P, N_TILE], F32, tag="bank")
+                for g in range(PASSES):
+                    nc.tensor.matmul_mx(
+                        out=out_ps[:],
+                        lhsT=y_codes[:, rt, P * g : P * (g + 1)].bitcast(FP8X4),
+                        lhsT_scale=y_scales[:, rt, P * g : P * (g + 1)],
+                        rhs=w_words[:, g, 2 * N_TILE * n : 2 * N_TILE * (n + 1)].bitcast(FP4X4),
+                        rhs_scale=w_scales[:, g, N_TILE * n : N_TILE * (n + 1)],
+                        start=(g == 0),
+                        stop=(g == PASSES - 1),
+                    )
+                copy = nc.vector.tensor_copy if n == 0 else nc.scalar.copy
+                copy(out=out_sb[:, N_TILE * n : N_TILE * (n + 1)], in_=out_ps[:])
+            nc.sync.dma_start(out=out_rows[P * rt : P * (rt + 1), :], in_=out_sb[:])
+
+        for step in range(ROW_TILES + AHEAD):
+            if step < ROW_TILES:
+                if step % (ROW_TILES // B) == 0:
+                    order_kv(step // (ROW_TILES // B))
+                transpose_q(step)
+            if step >= AHEAD:
+                read_out(step - AHEAD)
+            if step > AHEAD:
+                quantise(step - AHEAD - 1)
+        quantise(ROW_TILES - 1)
+
+        for rt in range(ROW_TILES):
+            project(rt)

@@ -25,6 +25,7 @@ ROW_GROUPS = S // 8 // SQUARE
 N_TILE = 512
 N_TILES = D // N_TILE
 AHEAD = 2
+BEHIND = 1
 
 FLOPS = 2 * B * H * S * DH * DH + 2 * B * S * D * D
 
@@ -37,28 +38,34 @@ def tile_mhla2_pb_kernel(tc, q_soft, kv, W_O_words, W_O_scales, out):
     with ExitStack() as ctx:
         keep = ctx.enter_context(tc.tile_pool(name="keep", bufs=1))
         stage = ctx.enter_context(tc.tile_pool(name="stage", bufs=3))
-        results = ctx.enter_context(tc.tile_pool(name="results", bufs=4))
+        results = ctx.enter_context(tc.tile_pool(name="results", bufs=6))
         banks = ctx.enter_context(tc.psum_pool(name="banks", bufs=8))
         ctx.enter_context(tc.manual_schedule())
 
         q_sb = keep.tile([P, HEADS, PACK, DH], BF16)
-        for rt in range(ROW_TILES):
-            heads = slice(TILE_HEADS * rt, TILE_HEADS * (rt + 1))
-            nc.sync.dma_start(out=q_sb[:, heads], in_=q_rows[:, heads])
         kv_sb = keep.tile([P, HEADS, DH], BF16)
-        for b in range(B):
-            nc.scalar.dma_start(out=kv_sb[:, H * b : H * (b + 1), :], in_=kv[b].rearrange("h d e -> d h e"))
-
         w_words = keep.tile([P, PASSES, 2 * D], U8, align_bytes=64)
-        nc.sync.dma_start(out=w_words[:].bitcast(I32), in_=W_O_words.bitcast(I32).rearrange("g p n -> p g n"))
         w_scales = keep.tile([P, PASSES, D], U8, align_bytes=64)
         nc.vector.memset(w_scales[:].bitcast(I32), 0)
-        scale_rows = W_O_scales.bitcast(I32).rearrange("g q n -> q g n")
-        for quadrant in range(P // SQUARE):
-            nc.sync.dma_start(
-                out=w_scales[SQUARE * quadrant : SQUARE * quadrant + PACK].bitcast(I32),
-                in_=scale_rows[PACK * quadrant : PACK * (quadrant + 1)],
-            )
+
+        def load_batch(b):
+            nc.scalar.dma_start(out=kv_sb[:, H * b : H * (b + 1), :], in_=kv[b].rearrange("h d e -> d h e"))
+            for first in range(H * b, H * (b + 1), TILE_HEADS):
+                heads = slice(first, first + TILE_HEADS)
+                nc.sync.dma_start(out=q_sb[:, heads], in_=q_rows[:, heads])
+
+        def load_w():
+            nc.sync.dma_start(out=w_words[:].bitcast(I32), in_=W_O_words.bitcast(I32).rearrange("g p n -> p g n"))
+            scale_rows = W_O_scales.bitcast(I32).rearrange("g q n -> q g n")
+            for quadrant in range(P // SQUARE):
+                nc.sync.dma_start(
+                    out=w_scales[SQUARE * quadrant : SQUARE * quadrant + PACK].bitcast(I32),
+                    in_=scale_rows[PACK * quadrant : PACK * (quadrant + 1)],
+                )
+
+        load_batch(0)
+        load_w()
+        load_batch(1)
 
         identity = keep.tile([P, P], BF16)
         make_identity(nc, identity[:])
@@ -122,7 +129,6 @@ def tile_mhla2_pb_kernel(tc, q_soft, kv, W_O_words, W_O_scales, out):
             )
 
         def project(rt):
-            out_sb = results.tile([P, D], F32)
             for n in range(N_TILES):
                 out_ps = banks.tile([P, N_TILE], F32, tag="bank")
                 for g in range(PASSES):
@@ -135,20 +141,18 @@ def tile_mhla2_pb_kernel(tc, q_soft, kv, W_O_words, W_O_scales, out):
                         start=(g == 0),
                         stop=(g == PASSES - 1),
                     )
-                copy = nc.vector.tensor_copy if n == 0 else nc.scalar.copy
-                copy(out=out_sb[:, N_TILE * n : N_TILE * (n + 1)], in_=out_ps[:])
-            nc.sync.dma_start(out=out_rows[P * rt : P * (rt + 1), :], in_=out_sb[:])
+                out_sb = results.tile([P, N_TILE], F32)
+                nc.scalar.copy(out=out_sb[:], in_=out_ps[:])
+                nc.sync.dma_start(out=out_rows[P * rt : P * (rt + 1), N_TILE * n : N_TILE * (n + 1)], in_=out_sb[:])
 
-        for step in range(ROW_TILES + AHEAD):
-            if step < ROW_TILES:
-                if step % (ROW_TILES // B) == 0:
-                    order_kv(step // (ROW_TILES // B))
-                transpose_q(step)
-            if step >= AHEAD:
-                read_out(step - AHEAD)
-            if step > AHEAD:
-                quantise(step - AHEAD - 1)
-        quantise(ROW_TILES - 1)
-
-        for rt in range(ROW_TILES):
-            project(rt)
+        for step in range(ROW_TILES + AHEAD + BEHIND):
+            front, middle, back = step, step - AHEAD, step - AHEAD - BEHIND
+            if front < ROW_TILES:
+                if front % (ROW_TILES // B) == 0:
+                    order_kv(front // (ROW_TILES // B))
+                transpose_q(front)
+            if 0 <= middle < ROW_TILES:
+                read_out(middle)
+                quantise(middle)
+            if back >= 0:
+                project(back)

@@ -24,8 +24,8 @@ ROW_TILES = HEADS // TILE_HEADS
 ROW_GROUPS = S // 8 // SQUARE
 N_TILE = 512
 N_TILES = D // N_TILE
-AHEAD = 2
-BEHIND = 1
+RUN = 2
+ROUNDS = ROW_TILES // RUN
 
 FLOPS = 2 * B * H * S * DH * DH + 2 * B * S * D * D
 
@@ -37,7 +37,7 @@ def tile_mhla2_pb_kernel(tc, q_soft, kv, W_O_words, W_O_scales, out):
 
     with ExitStack() as ctx:
         keep = ctx.enter_context(tc.tile_pool(name="keep", bufs=1))
-        stage = ctx.enter_context(tc.tile_pool(name="stage", bufs=3))
+        stage = ctx.enter_context(tc.tile_pool(name="stage", bufs=2 * RUN))
         results = ctx.enter_context(tc.tile_pool(name="results", bufs=6))
         banks = ctx.enter_context(tc.psum_pool(name="banks", bufs=8))
         ctx.enter_context(tc.manual_schedule())
@@ -79,6 +79,7 @@ def tile_mhla2_pb_kernel(tc, q_soft, kv, W_O_words, W_O_scales, out):
         y_codes = keep.tile([P, ROW_TILES, PASSES * P], U32, align_bytes=64)
         y_scales = keep.tile([P, ROW_TILES, PASSES * P], U8, align_bytes=64)
         q_t = {}
+        turned = {}
         grouped = {}
 
         def order_kv(b):
@@ -98,7 +99,7 @@ def tile_mhla2_pb_kernel(tc, q_soft, kv, W_O_words, W_O_scales, out):
                         identity=order[:],
                     )
             q_t[rt] = stage.tile([P, TILE_HEADS, PASSES * ROW_GROUPS, P], BF16, name="q_t_sb")
-            nc.scalar.copy(
+            nc.vector.tensor_copy(
                 out=q_t[rt][:].rearrange("d h o m -> d (h o m)"),
                 in_=q_t_ps[:].rearrange("d h o x i -> d (h o x i)"),
             )
@@ -115,12 +116,14 @@ def tile_mhla2_pb_kernel(tc, q_soft, kv, W_O_words, W_O_scales, out):
                             start=True,
                             stop=True,
                         )
-            turned = stage.tile([P, PASSES * P * 2], F32, align_bytes=64)
-            nc.vector.transpose(out=turned[:], in_=y_ps[:].rearrange("m g h j n -> m (g h j n)").bitcast(F32))
+            turned[rt] = stage.tile([P, PASSES * P * 2], F32, name="turned", align_bytes=64)
+            nc.vector.transpose(out=turned[rt][:], in_=y_ps[:].rearrange("m g h j n -> m (g h j n)").bitcast(F32))
+
+        def group(rt):
             grouped[rt] = stage.tile([P, PASSES * P * PACK], BF16, name="grouped", align_bytes=64)
             nc.vector.tensor_copy(
                 out=grouped[rt][:].bitcast(F32).rearrange("p (o i u) -> p o i u", i=SQUARE, u=2),
-                in_=turned[:].rearrange("p (o u i) -> p o i u", i=SQUARE, u=2),
+                in_=turned[rt][:].rearrange("p (o u i) -> p o i u", i=SQUARE, u=2),
             )
 
         def quantise(rt):
@@ -145,14 +148,19 @@ def tile_mhla2_pb_kernel(tc, q_soft, kv, W_O_words, W_O_scales, out):
                 nc.scalar.copy(out=out_sb[:], in_=out_ps[:])
                 nc.sync.dma_start(out=out_rows[P * rt : P * (rt + 1), N_TILE * n : N_TILE * (n + 1)], in_=out_sb[:])
 
-        for step in range(ROW_TILES + AHEAD + BEHIND):
-            front, middle, back = step, step - AHEAD, step - AHEAD - BEHIND
-            if front < ROW_TILES:
-                if front % (ROW_TILES // B) == 0:
-                    order_kv(front // (ROW_TILES // B))
-                transpose_q(front)
-            if 0 <= middle < ROW_TILES:
-                read_out(middle)
-                quantise(middle)
-            if back >= 0:
-                project(back)
+        def row_tiles(turn):
+            return range(RUN * turn, RUN * (turn + 1)) if 0 <= turn < ROUNDS else ()
+
+        for step in range(ROUNDS + 2):
+            for rt in row_tiles(step):
+                if rt % (ROW_TILES // B) == 0:
+                    order_kv(rt // (ROW_TILES // B))
+                transpose_q(rt)
+            for rt in row_tiles(step - 1):
+                read_out(rt)
+            for rt in row_tiles(step - 1):
+                group(rt)
+            for rt in row_tiles(step - 1):
+                quantise(rt)
+            for rt in row_tiles(step - 2):
+                project(rt)

@@ -48,11 +48,13 @@ def tile_mhla2_pb_kernel(tc, q_soft, kv, W_O_words, W_O_scales, out):
         w_scales = keep.tile([P, PASSES, D], U8, align_bytes=64)
         nc.vector.memset(w_scales[:].bitcast(I32), 0)
 
-        def load_batch(b):
-            nc.scalar.dma_start(out=kv_sb[:, H * b : H * (b + 1), :], in_=kv[b].rearrange("h d e -> d h e"))
-            for first in range(H * b, H * (b + 1), TILE_HEADS):
-                heads = slice(first, first + TILE_HEADS)
+        def load_q(turn):
+            for rt in range(RUN * turn, RUN * (turn + 1)):
+                heads = slice(TILE_HEADS * rt, TILE_HEADS * (rt + 1))
                 nc.sync.dma_start(out=q_sb[:, heads], in_=q_rows[:, heads])
+
+        def load_kv(b):
+            nc.sync.dma_start(out=kv_sb[:, H * b : H * (b + 1), :], in_=kv[b].rearrange("h d e -> d h e"))
 
         def load_w():
             nc.sync.dma_start(out=w_words[:].bitcast(I32), in_=W_O_words.bitcast(I32).rearrange("g p n -> p g n"))
@@ -63,9 +65,13 @@ def tile_mhla2_pb_kernel(tc, q_soft, kv, W_O_words, W_O_scales, out):
                     in_=scale_rows[PACK * quadrant : PACK * (quadrant + 1)],
                 )
 
-        load_batch(0)
+        load_q(0)
+        load_q(1)
+        load_kv(0)
+        load_q(2)
         load_w()
-        load_batch(1)
+        load_q(3)
+        load_kv(1)
 
         identity = keep.tile([P, P], BF16)
         make_identity(nc, identity[:])
@@ -152,9 +158,10 @@ def tile_mhla2_pb_kernel(tc, q_soft, kv, W_O_words, W_O_scales, out):
             return range(RUN * turn, RUN * (turn + 1)) if 0 <= turn < ROUNDS else ()
 
         for step in range(ROUNDS + 2):
-            for rt in row_tiles(step):
+            for rt in row_tiles(step - 1):
                 if rt % (ROW_TILES // B) == 0:
                     order_kv(rt // (ROW_TILES // B))
+            for rt in row_tiles(step):
                 transpose_q(rt)
             for rt in row_tiles(step - 1):
                 read_out(rt)

@@ -105,7 +105,7 @@ def tile_mhla2_pb_kernel(tc, q_soft, kv, W_O_words, W_O_scales, out):
                         identity=order[:],
                     )
             q_t[rt] = stage.tile([P, TILE_HEADS, PASSES * ROW_GROUPS, P], BF16, name="q_t_sb")
-            nc.vector.tensor_copy(
+            nc.scalar.copy(
                 out=q_t[rt][:].rearrange("d h o m -> d (h o m)"),
                 in_=q_t_ps[:].rearrange("d h o x i -> d (h o x i)"),
             )

@@ -26,6 +26,7 @@ N_TILE = 512
 N_TILES = D // N_TILE
 RUN = 2
 ROUNDS = ROW_TILES // RUN
+WARM_UP = 5
 
 FLOPS = 2 * B * H * S * DH * DH + 2 * B * S * D * D
 
@@ -46,7 +47,12 @@ def tile_mhla2_pb_kernel(tc, q_soft, kv, W_O_words, W_O_scales, out):
         kv_sb = keep.tile([P, HEADS, DH], BF16)
         w_words = keep.tile([P, PASSES, 2 * D], U8, align_bytes=64)
         w_scales = keep.tile([P, PASSES, D], U8, align_bytes=64)
+        zeros = keep.tile([P, N_TILE], BF16)
+        nc.vector.memset(zeros[:], 0.0)
         nc.vector.memset(w_scales[:].bitcast(I32), 0)
+        warm_ps = banks.tile([P, N_TILE], F32, tag="bank")
+        for i in range(WARM_UP):
+            nc.tensor.matmul(out=warm_ps[:], lhsT=zeros[:, :P], rhs=zeros[:], start=True, stop=True)
 
         def load_q(turn):
             for rt in range(RUN * turn, RUN * (turn + 1)):

@@ -24,6 +24,7 @@ ROW_TILES = HEADS // TILE_HEADS
 ROW_GROUPS = S // 8 // SQUARE
 N_TILE = 512
 N_TILES = D // N_TILE
+ROW = D // DH
 RUN = 2
 ROUNDS = ROW_TILES // RUN
 WARM_UP = 5
@@ -33,7 +34,7 @@ FLOPS = 2 * B * H * S * DH * DH + 2 * B * S * D * D
 
 def tile_mhla2_pb_kernel(tc, q_soft, kv, W_O_words, W_O_scales, out):
     nc = tc.nc
-    q_rows = q_soft.rearrange("b h (a x) d -> a (b h) x d", x=PACK)
+    q_rows = q_soft.rearrange("b (c h) (r s) d -> (h r) (b c) (s d)", h=TILE_HEADS, s=ROW)
     out_rows = out.rearrange("b r o -> (b r) o")
 
     with ExitStack() as ctx:
@@ -43,7 +44,7 @@ def tile_mhla2_pb_kernel(tc, q_soft, kv, W_O_words, W_O_scales, out):
         banks = ctx.enter_context(tc.psum_pool(name="banks", bufs=8))
         ctx.enter_context(tc.manual_schedule())
 
-        q_sb = keep.tile([P, HEADS, PACK, DH], BF16)
+        q_sb = keep.tile([P, ROW_TILES, ROW, DH], BF16)
         kv_sb = keep.tile([P, HEADS, DH], BF16)
         w_words = keep.tile([P, PASSES, 2 * D], U8, align_bytes=64)
         w_scales = keep.tile([P, PASSES, D], U8, align_bytes=64)
@@ -56,8 +57,7 @@ def tile_mhla2_pb_kernel(tc, q_soft, kv, W_O_words, W_O_scales, out):
 
         def load_q(turn):
             for rt in range(RUN * turn, RUN * (turn + 1)):
-                heads = slice(TILE_HEADS * rt, TILE_HEADS * (rt + 1))
-                nc.sync.dma_start(out=q_sb[:, heads], in_=q_rows[:, heads])
+                nc.sync.dma_start(out=q_sb[:, rt].rearrange("a s d -> a (s d)"), in_=q_rows[:, rt])
 
         def load_kv(b):
             nc.sync.dma_start(out=kv_sb[:, H * b : H * (b + 1), :], in_=kv[b].rearrange("h d e -> d h e"))
@@ -81,39 +81,26 @@ def tile_mhla2_pb_kernel(tc, q_soft, kv, W_O_words, W_O_scales, out):
 
         identity = keep.tile([P, P], BF16)
         make_identity(nc, identity[:])
-        order = keep.tile([P, P], BF16)
-        nc.vector.tensor_copy(
-            out=order[:].rearrange("a (g j i) -> a g j i", g=PASSES, j=ROW_GROUPS),
-            in_=identity[:].rearrange("a (j i g) -> a g j i", g=PASSES, j=ROW_GROUPS),
-        )
 
-        kv_pairs = keep.tile([P, HEADS, DH], BF16)
         y_codes = keep.tile([P, ROW_TILES, PASSES * P], U32, align_bytes=64)
         y_scales = keep.tile([P, ROW_TILES, PASSES * P], U8, align_bytes=64)
         q_t = {}
         turned = {}
         grouped = {}
 
-        def order_kv(b):
-            heads = slice(H * b, H * (b + 1))
-            nc.vector.tensor_copy(
-                out=kv_pairs[:, heads, :].bitcast(F32).rearrange("d h (u c) -> d h u c", u=2),
-                in_=kv_sb[:, heads, :].bitcast(F32).rearrange("d h (c u) -> d h u c", u=2),
-            )
-
         def transpose_q(rt):
-            q_t_ps = banks.tile([P, TILE_HEADS, PASSES * ROW_GROUPS, PACK, SQUARE], BF16, tag="bank")
-            for h in range(TILE_HEADS):
+            q_t_ps = banks.tile([P, PASSES, TILE_HEADS * ROW_GROUPS, PACK, SQUARE], BF16, tag="bank")
+            for g in range(PASSES):
                 for x in range(PACK):
                     nc.tensor.transpose(
-                        out=q_t_ps[:, h, :, x, :],
-                        in_=q_sb[:, TILE_HEADS * rt + h, x, :],
-                        identity=order[:],
+                        out=q_t_ps[:, g, :, x, :],
+                        in_=q_sb[:, rt, PACK * g + x, :],
+                        identity=identity[:],
                     )
-            q_t[rt] = stage.tile([P, TILE_HEADS, PASSES * ROW_GROUPS, P], BF16, name="q_t_sb")
+            q_t[rt] = stage.tile([P, PASSES, TILE_HEADS * ROW_GROUPS, P], BF16, name="q_t_sb")
             nc.scalar.copy(
-                out=q_t[rt][:].rearrange("d h o m -> d (h o m)"),
-                in_=q_t_ps[:].rearrange("d h o x i -> d (h o x i)"),
+                out=q_t[rt][:].rearrange("d g o m -> d (g o m)"),
+                in_=q_t_ps[:].rearrange("d g o x i -> d (g o x i)"),
             )
 
         def read_out(rt):
@@ -122,9 +109,9 @@ def tile_mhla2_pb_kernel(tc, q_soft, kv, W_O_words, W_O_scales, out):
                 for g in range(PASSES):
                     for j in range(ROW_GROUPS):
                         nc.tensor.matmul(
-                            out=y_ps[:, g, h, j, :],
-                            lhsT=q_t[rt][:, h, ROW_GROUPS * g + j, :],
-                            rhs=kv_pairs[:, TILE_HEADS * rt + h, :],
+                            out=y_ps[:, g, h, j, :].rearrange("m (u c t) -> m u c t", u=2, t=2),
+                            lhsT=q_t[rt][:, g, ROW_GROUPS * h + j, :],
+                            rhs=kv_sb[:, TILE_HEADS * rt + h, :].rearrange("d (c u t) -> d u c t", u=2, t=2),
                             start=True,
                             stop=True,
                         )
@@ -164,9 +151,6 @@ def tile_mhla2_pb_kernel(tc, q_soft, kv, W_O_words, W_O_scales, out):
             return range(RUN * turn, RUN * (turn + 1)) if 0 <= turn < ROUNDS else ()
 
         for step in range(ROUNDS + 2):
-            for rt in row_tiles(step - 1):
-                if rt % (ROW_TILES // B) == 0:
-                    order_kv(rt // (ROW_TILES // B))
             for rt in row_tiles(step):
                 transpose_q(rt)
             for rt in row_tiles(step - 1):

@@ -27,7 +27,7 @@ N_TILES = D // N_TILE
 ROW = D // DH
 RUN = 2
 ROUNDS = ROW_TILES // RUN
-WARM_UP = 5
+WARM_UP = 16
 
 FLOPS = 2 * B * H * S * DH * DH + 2 * B * S * D * D
 
@@ -48,16 +48,21 @@ def tile_mhla2_pb_kernel(tc, q_soft, kv, W_O_words, W_O_scales, out):
         kv_sb = keep.tile([P, HEADS, DH], BF16)
         w_words = keep.tile([P, PASSES, 2 * D], U8, align_bytes=64)
         w_scales = keep.tile([P, PASSES, D], U8, align_bytes=64)
-        zeros = keep.tile([P, N_TILE], BF16)
+        zeros = keep.tile([P, P], BF16)
         nc.vector.memset(zeros[:], 0.0)
         nc.vector.memset(w_scales[:].bitcast(I32), 0)
-        warm_ps = banks.tile([P, N_TILE], F32, tag="bank")
+        warm_ps = banks.tile([P, P], F32, tag="bank")
         for i in range(WARM_UP):
-            nc.tensor.matmul(out=warm_ps[:], lhsT=zeros[:, :P], rhs=zeros[:], start=True, stop=True)
+            nc.tensor.matmul(out=warm_ps[:], lhsT=zeros[:], rhs=zeros[:], start=True, stop=True)
 
         def load_q(turn):
             for rt in range(RUN * turn, RUN * (turn + 1)):
-                nc.sync.dma_start(out=q_sb[:, rt].rearrange("a s d -> a (s d)"), in_=q_rows[:, rt])
+                rows = ROW if rt else PACK
+                for s in range(0, ROW, rows):
+                    nc.sync.dma_start(
+                        out=q_sb[:, rt, s : s + rows].rearrange("a s d -> a (s d)"),
+                        in_=q_rows[:, rt, DH * s : DH * (s + rows)],
+                    )
 
         def load_kv(b):
             nc.sync.dma_start(out=kv_sb[:, H * b : H * (b + 1), :], in_=kv[b].rearrange("h d e -> d h e"))

@@ -27,6 +27,7 @@ N_TILES = D // N_TILE
 ROW = D // DH
 RUN = 2
 ROUNDS = ROW_TILES // RUN
+LEAD = 3
 WARM_UP = 16
 
 FLOPS = 2 * B * H * S * DH * DH + 2 * B * S * D * D
@@ -80,9 +81,9 @@ def tile_mhla2_pb_kernel(tc, q_soft, kv, W_O_words, W_O_scales, out):
         load_q(1)
         load_kv(0)
         load_q(2)
-        load_w()
         load_q(3)
         load_kv(1)
+        load_w()
 
         identity = keep.tile([P, P], BF16)
         make_identity(nc, identity[:])
@@ -153,16 +154,23 @@ def tile_mhla2_pb_kernel(tc, q_soft, kv, W_O_words, W_O_scales, out):
                 nc.sync.dma_start(out=out_rows[P * rt : P * (rt + 1), N_TILE * n : N_TILE * (n + 1)], in_=out_sb[:])
 
         def row_tiles(turn):
-            return range(RUN * turn, RUN * (turn + 1)) if 0 <= turn < ROUNDS else ()
+            return range(RUN * turn, RUN * (turn + 1))
 
-        for step in range(ROUNDS + 2):
-            for rt in row_tiles(step):
-                transpose_q(rt)
-            for rt in row_tiles(step - 1):
+        def carry_y(tiles):
+            for rt in tiles:
                 read_out(rt)
-            for rt in row_tiles(step - 1):
+            for rt in tiles:
                 group(rt)
-            for rt in row_tiles(step - 1):
+            for rt in tiles:
                 quantise(rt)
-            for rt in row_tiles(step - 2):
-                project(rt)
+
+        for rt in row_tiles(0):
+            transpose_q(rt)
+        for turn in range(1, ROUNDS):
+            for rt in row_tiles(turn):
+                transpose_q(rt)
+            carry_y(row_tiles(turn - 1))
+        for rt in range(ROW_TILES):
+            project(rt)
+            if rt + LEAD in row_tiles(ROUNDS - 1):
+                carry_y((rt + LEAD,))

from contextlib import ExitStack

import concourse.mybir as mybir
from concourse.masks import make_identity

BF16 = mybir.dt.bfloat16
F32 = mybir.dt.float32
I32 = mybir.dt.int32
U8 = mybir.dt.uint8
U32 = mybir.dt.uint32
FP8X4 = mybir.dt.float8_e4m3fn_x4
FP4X4 = mybir.dt.float4_e2m1fn_x4

B, H, S, DH = 2, 8, 512, 128
D = H * DH

P = 128
PACK = 4
PASSES = D // (P * PACK)
SQUARE = 32
HEADS = B * H
TILE_HEADS = 2
ROW_TILES = HEADS // TILE_HEADS
ROW_GROUPS = S // 8 // SQUARE
N_TILE = 512
N_TILES = D // N_TILE
ROW = D // DH
RUN = 2
ROUNDS = ROW_TILES // RUN
LEAD = 3
WARM_UP = 16

FLOPS = 2 * B * H * S * DH * DH + 2 * B * S * D * D


def tile_mhla2_pb_kernel(tc, q_soft, kv, W_O_words, W_O_scales, out):
    nc = tc.nc
    q_rows = q_soft.rearrange("b (c h) (r s) d -> (h r) (b c) (s d)", h=TILE_HEADS, s=ROW)
    out_rows = out.rearrange("b r o -> (b r) o")

    with ExitStack() as ctx:
        keep = ctx.enter_context(tc.tile_pool(name="keep", bufs=1))
        stage = ctx.enter_context(tc.tile_pool(name="stage", bufs=2 * RUN))
        results = ctx.enter_context(tc.tile_pool(name="results", bufs=6))
        banks = ctx.enter_context(tc.psum_pool(name="banks", bufs=8))
        ctx.enter_context(tc.manual_schedule())

        q_sb = keep.tile([P, ROW_TILES, ROW, DH], BF16)
        kv_sb = keep.tile([P, HEADS, DH], BF16)
        w_words = keep.tile([P, PASSES, 2 * D], U8, align_bytes=64)
        w_scales = keep.tile([P, PASSES, D], U8, align_bytes=64)
        zeros = keep.tile([P, P], BF16)
        nc.vector.memset(zeros[:], 0.0)
        nc.vector.memset(w_scales[:].bitcast(I32), 0)
        warm_ps = banks.tile([P, P], F32, tag="bank")
        for i in range(WARM_UP):
            nc.tensor.matmul(out=warm_ps[:], lhsT=zeros[:], rhs=zeros[:], start=True, stop=True)

        def load_q(turn):
            for rt in range(RUN * turn, RUN * (turn + 1)):
                rows = ROW if rt else PACK
                for s in range(0, ROW, rows):
                    nc.sync.dma_start(
                        out=q_sb[:, rt, s : s + rows].rearrange("a s d -> a (s d)"),
                        in_=q_rows[:, rt, DH * s : DH * (s + rows)],
                    )

        def load_kv(b):
            nc.sync.dma_start(out=kv_sb[:, H * b : H * (b + 1), :], in_=kv[b].rearrange("h d e -> d h e"))

        def load_w():
            nc.sync.dma_start(out=w_words[:].bitcast(I32), in_=W_O_words.bitcast(I32).rearrange("g p n -> p g n"))
            scale_rows = W_O_scales.bitcast(I32).rearrange("g q n -> q g n")
            for quadrant in range(P // SQUARE):
                nc.sync.dma_start(
                    out=w_scales[SQUARE * quadrant : SQUARE * quadrant + PACK].bitcast(I32),
                    in_=scale_rows[PACK * quadrant : PACK * (quadrant + 1)],
                )

        load_q(0)
        load_q(1)
        load_kv(0)
        load_q(2)
        load_q(3)
        load_kv(1)
        load_w()

        identity = keep.tile([P, P], BF16)
        make_identity(nc, identity[:])

        y_codes = keep.tile([P, ROW_TILES, PASSES * P], U32, align_bytes=64)
        y_scales = keep.tile([P, ROW_TILES, PASSES * P], U8, align_bytes=64)
        q_t = {}
        turned = {}
        grouped = {}

        def transpose_q(rt):
            q_t_ps = banks.tile([P, PASSES, TILE_HEADS * ROW_GROUPS, PACK, SQUARE], BF16, tag="bank")
            for g in range(PASSES):
                for x in range(PACK):
                    nc.tensor.transpose(
                        out=q_t_ps[:, g, :, x, :],
                        in_=q_sb[:, rt, PACK * g + x, :],
                        identity=identity[:],
                    )
            q_t[rt] = stage.tile([P, PASSES, TILE_HEADS * ROW_GROUPS, P], BF16, name="q_t_sb")
            nc.scalar.copy(
                out=q_t[rt][:].rearrange("d g o m -> d (g o m)"),
                in_=q_t_ps[:].rearrange("d g o x i -> d (g o x i)"),
            )

        def read_out(rt):
            y_ps = banks.tile([P, PASSES, TILE_HEADS, ROW_GROUPS, DH], BF16, tag="bank")
            for h in range(TILE_HEADS):
                for g in range(PASSES):
                    for j in range(ROW_GROUPS):
                        nc.tensor.matmul(
                            out=y_ps[:, g, h, j, :].rearrange("m (u c t) -> m u c t", u=2, t=2),
                            lhsT=q_t[rt][:, g, ROW_GROUPS * h + j, :],
                            rhs=kv_sb[:, TILE_HEADS * rt + h, :].rearrange("d (c u t) -> d u c t", u=2, t=2),
                            start=True,
                            stop=True,
                        )
            turned[rt] = stage.tile([P, PASSES * P * 2], F32, name="turned", align_bytes=64)
            nc.vector.transpose(out=turned[rt][:], in_=y_ps[:].rearrange("m g h j n -> m (g h j n)").bitcast(F32))

        def group(rt):
            grouped[rt] = stage.tile([P, PASSES * P * PACK], BF16, name="grouped", align_bytes=64)
            nc.vector.tensor_copy(
                out=grouped[rt][:].bitcast(F32).rearrange("p (o i u) -> p o i u", i=SQUARE, u=2),
                in_=turned[rt][:].rearrange("p (o u i) -> p o i u", i=SQUARE, u=2),
            )

        def quantise(rt):
            nc.vector.quantize_mx(
                out=y_codes[:, rt, :].bitcast(FP8X4), scales=y_scales[:, rt, :], in_=grouped[rt][:]
            )

        def project(rt):
            for n in range(N_TILES):
                out_ps = banks.tile([P, N_TILE], F32, tag="bank")
                for g in range(PASSES):
                    nc.tensor.matmul_mx(
                        out=out_ps[:],
                        lhsT=y_codes[:, rt, P * g : P * (g + 1)].bitcast(FP8X4),
                        lhsT_scale=y_scales[:, rt, P * g : P * (g + 1)],
                        rhs=w_words[:, g, 2 * N_TILE * n : 2 * N_TILE * (n + 1)].bitcast(FP4X4),
                        rhs_scale=w_scales[:, g, N_TILE * n : N_TILE * (n + 1)],
                        start=(g == 0),
                        stop=(g == PASSES - 1),
                    )
                out_sb = results.tile([P, N_TILE], F32)
                nc.scalar.copy(out=out_sb[:], in_=out_ps[:])
                nc.sync.dma_start(out=out_rows[P * rt : P * (rt + 1), N_TILE * n : N_TILE * (n + 1)], in_=out_sb[:])

        def row_tiles(turn):
            return range(RUN * turn, RUN * (turn + 1))

        def carry_y(tiles):
            for rt in tiles:
                read_out(rt)
            for rt in tiles:
                group(rt)
            for rt in tiles:
                quantise(rt)

        for rt in row_tiles(0):
            transpose_q(rt)
        for turn in range(1, ROUNDS):
            for rt in row_tiles(turn):
                transpose_q(rt)
            carry_y(row_tiles(turn - 1))
        for rt in range(ROW_TILES):
            project(rt)
            if rt + LEAD in row_tiles(ROUNDS - 1):
                carry_y((rt + LEAD,))
